import numpy as np
import ml_dtypes


def mxq(x, axis, fmt="e4m3"):
    dtype, down = {"e4m3": (ml_dtypes.float8_e4m3fn, 7), "e5m2": (ml_dtypes.float8_e5m2, 14)}[fmt]
    v = np.moveaxis(np.asarray(x, np.float32).astype(ml_dtypes.bfloat16).astype(np.float64), axis, -1)
    blocks = v.reshape(v.shape[:-1] + (-1, 32))
    amax = np.abs(blocks).max(-1, keepdims=True)
    byte = np.maximum(np.where(amax > 0, np.frexp(amax)[1] - 1 + 127, 0) - down, 1)
    scale = np.exp2(byte - 127.0)
    codes = (blocks / scale).astype(np.float32).astype(dtype).astype(np.float64)
    return np.moveaxis((codes * scale).reshape(v.shape), -1, axis)


WIDE = False


def mx_kscale(k):
    if not WIDE:
        return np.ones(k)
    levels = np.array([30, -30])
    if k % 512:
        return np.exp2(np.random.permutation(np.resize(levels, k // 32))).repeat(32)
    a = np.empty((k // 512, 16))
    for p in range(k // 512):
        a[p, :8] = np.random.permutation(np.resize(levels, 8))
        for g in range(8):
            far = levels[np.abs(levels - a[p, g]) >= 10]
            a[p, g + 8] = far[np.random.randint(len(far))]
    return np.exp2(a.ravel()).repeat(32)


BF16 = ml_dtypes.bfloat16


def bf(x):
    return np.asarray(x, np.float32).astype(BF16)


def f64(x):
    return np.asarray(x).astype(np.float64)


E2M1 = np.array([0.0, 0.5, 1.0, 1.5, 2.0, 3.0, 4.0, 6.0, -0.0, -0.5, -1.0, -1.5, -2.0, -3.0, -4.0, -6.0])


def pack_weight(w, fmt):
    k, n = w.shape
    w = f64(bf(w)).reshape(k // 32, 32, n)
    amax = np.abs(w).max(1)
    if fmt == "e4m3":
        byte = np.frexp(amax)[1] - 1 + 127 - 7
    else:
        mant, ex = np.frexp(amax / 6.0)
        byte = np.where(mant > 0.5, ex, ex - 1) + 127
    byte = np.clip(np.where(amax > 0, byte, 1), 1, 254)
    scaled = (w * np.exp2(127.0 - byte)[:, None, :]).reshape(k, n).astype(np.float32)
    by_word = np.ascontiguousarray(scaled.reshape(k // 512, 128, 4, n).transpose(0, 1, 3, 2))
    if fmt == "e4m3":
        words = by_word.astype(ml_dtypes.float8_e4m3fn).view(np.uint8)
    else:
        c = by_word.astype(ml_dtypes.float4_e2m1fn).view(np.uint8) & 0xF
        words = c[..., 0::2] | (c[..., 1::2] << 4)
    return np.ascontiguousarray(words), np.ascontiguousarray(byte.astype(np.uint8).reshape(k // 512, 16, n))


def unpack_weight(words, scales, fmt):
    g, p, n, _ = words.shape
    if fmt == "e4m3":
        vals = np.ascontiguousarray(words).view(ml_dtypes.float8_e4m3fn).astype(np.float64)
    else:
        nib = np.empty((g, p, n, 4), np.uint8)
        nib[..., 0::2] = words & 0xF
        nib[..., 1::2] = words >> 4
        vals = E2M1[nib]
    vals = vals * np.repeat(np.exp2(scales.astype(np.float64) - 127.0), 8, axis=1)[..., None]
    return vals.transpose(0, 1, 3, 2).reshape(g * 512, n)

def pack4(w):
    words, scales = pack_weight(w, "e2m1")
    return words.reshape(words.shape[0], 128, -1), scales


def unpack4(words, scales):
    return unpack_weight(words.reshape(words.shape[0], 128, -1, 2), scales, "e2m1")


B, S, D, NH, NKV, HD = 2, 256, 2048, 16, 4, 128
EPS = 1e-6
QS = NH * HD
KS = NKV * HD
E = QS + KS + KS
HP = HD // 2


def rmsnorm(v, w):
    ms = np.mean(np.square(v), axis=-1, keepdims=True)
    return v * (1.0 / np.sqrt(ms + EPS)) * w


def apply_rotary_emb(v, fc):
    vs = v.reshape(*v.shape[:-1], HP, 2)
    f = fc[None, :, None, :, :]
    vr, vi = vs[..., 0], vs[..., 1]
    fr, fi = f[..., 0], f[..., 1]
    return np.stack([vr * fr - vi * fi, vi * fr + vr * fi], axis=-1).reshape(v.shape)


def setup_inputs():
    s = mx_kscale(D)
    x = bf(np.random.standard_normal((B, S, D)) * s)
    freqs_cis = bf(np.random.standard_normal((S, HP, 2)))
    wqkv = np.random.standard_normal((E, D)) / np.sqrt(D) / s[None, :]
    words, scales = pack4(np.ascontiguousarray(wqkv.T))
    q_norm_w = bf(1.0 + 0.1 * np.random.standard_normal(HD))
    k_norm_w = bf(1.0 + 0.1 * np.random.standard_normal(HD))
    return {"x": x,
            "freqs_cis": freqs_cis,
            "wqkv_words": words,
            "wqkv_scales": scales,
            "q_norm_w": q_norm_w,
            "k_norm_w": k_norm_w}


def reference(x, freqs_cis, wqkv_words, wqkv_scales, q_norm_w, k_norm_w):
    fc = f64(freqs_cis)
    qkv = mxq(f64(x), 2, "e5m2") @ unpack4(wqkv_words, wqkv_scales)
    q = qkv[..., :QS].reshape(B, S, NH, HD)
    k = qkv[..., QS:QS + KS].reshape(B, S, NKV, HD)
    v = qkv[..., QS + KS:].reshape(B, S, NKV, HD)
    q = rmsnorm(q, f64(q_norm_w))
    k = rmsnorm(k, f64(k_norm_w))
    q_rot = apply_rotary_emb(q, fc)
    k_rot = apply_rotary_emb(k, fc)
    return q_rot, k_rot, v

@@ -1,0 +1,201 @@
+from contextlib import ExitStack
+
+import concourse.mybir as mybir
+from concourse.masks import make_identity
+
+B, S, D, NH, NKV, HD = 2, 256, 2048, 16, 4, 128
+E = (NH + 2 * NKV) * HD
+EPS = 1e-6
+FLOPS = 2 * B * S * D * E
+
+F32 = mybir.dt.float32
+BF16 = mybir.dt.bfloat16
+I32 = mybir.dt.int32
+U32 = mybir.dt.uint32
+U8 = mybir.dt.uint8
+E5M2X4 = mybir.dt.float8_e5m2_x4
+E2M1X4 = mybir.dt.float4_e2m1fn_x4
+ACT = mybir.ActivationFunctionType
+ALU = mybir.AluOpType
+
+P = 128
+PASSES = D // 512
+CHUNK = 512
+CHUNKS = E // CHUNK
+Q_CHUNKS = NH * HD // CHUNK
+V_CHUNK = CHUNKS - 1
+HEADS = CHUNK // HD
+TILES = B * S // P
+HALVES = S // P
+PAIRS = HD // 2
+
+
+def tile_attention_pa_kernel(tc, x, freqs_cis, wqkv_words, wqkv_scales, q_norm_w, k_norm_w, out_0, out_1, out_2):
+    nc = tc.nc
+    x_rows = x.rearrange("b s d -> (b s) d")
+    outs = [o.rearrange("b s h d -> (b s) (h d)") for o in (out_0, out_1, out_2)]
+
+    with ExitStack() as ctx:
+        keep = ctx.enter_context(tc.tile_pool(name="keep", bufs=1))
+        work = ctx.enter_context(tc.tile_pool(name="work", bufs=4))
+        psum = ctx.enter_context(tc.psum_pool(name="psum", bufs=8))
+        ctx.enter_context(tc.manual_schedule())
+
+        ident = keep.tile([P, P], F32, name="ident")
+        make_identity(nc, ident[:])
+
+        first_plane = keep.tile([P, PASSES, CHUNK], U8, name="first_plane", align_bytes=64)
+        rest_plane = keep.tile([P, PASSES, E - CHUNK], U8, name="rest_plane", align_bytes=64)
+        gain_rows = keep.tile([P, 2 * HD], BF16, name="gain_rows")
+        ones = keep.tile([P, P], BF16, name="ones")
+        nc.vector.memset(first_plane[:].bitcast(I32), 0)
+        nc.vector.memset(gain_rows[:], 0.0)
+        nc.vector.memset(ones[:], 1.0)
+        nc.vector.memset(rest_plane[:].bitcast(I32), 0)
+
+        eps = keep.tile([P, 1], F32, name="eps")
+        nc.scalar.activation(out=eps[:], in_=ones[:, 0:1], func=ACT.Abs_reciprocal_sqrt, scale=1.0 / (EPS * EPS))
+
+        x_sb = {}
+        w_sb = {}
+
+        def load_x(t, pieces):
+            width = D // pieces
+            for i in range(pieces):
+                piece = keep.tile([P, width], BF16, name="x_%d_%d" % (t, i))
+                nc.sync.dma_start(out=piece[:], in_=x_rows[P * t : P * (t + 1), width * i : width * (i + 1)])
+                for j in range(width // 1024):
+                    x_sb[t, i * (width // 1024) + j] = piece[:, 1024 * j : 1024 * (j + 1)]
+
+        def load_w(c):
+            w_sb[c] = keep.tile([P, PASSES, 2 * CHUNK], U8, name="w_%d" % c, align_bytes=64)
+            src = wqkv_words[:, :, 2 * CHUNK * c : 2 * CHUNK * (c + 1)].rearrange("g p n -> p g n")
+            nc.sync.dma_start(out=w_sb[c][:].bitcast(I32), in_=src.bitcast(I32))
+
+        def load_scales(plane, cols):
+            for r in range(4):
+                src = wqkv_scales[:, r:16:4, cols].rearrange("g q n -> q g n")
+                nc.sync.dma_start(out=plane[r:P:32, :, :].bitcast(I32), in_=src.bitcast(I32))
+
+        freqs = keep.tile([P, 2, HALVES, PAIRS, 2], BF16, name="freqs")
+
+        load_x(0, 2)
+        load_w(0)
+        load_scales(first_plane, slice(0, CHUNK))
+        nc.sync.dma_start(out=gain_rows[0:1, 0:HD], in_=q_norm_w.rearrange("(o d) -> o d", o=1))
+        nc.sync.dma_start(out=gain_rows[0:1, HD : 2 * HD], in_=k_norm_w.rearrange("(o d) -> o d", o=1))
+        nc.sync.dma_start(out=freqs[:, 0], in_=freqs_cis.rearrange("(h p) j e -> p h j e", p=P))
+        for t in range(1, TILES):
+            load_x(t, 1)
+        load_scales(rest_plane, slice(CHUNK, E))
+        for c in range(1, CHUNKS):
+            load_w(c)
+
+        codes = {}
+        x_scales = {}
+
+        def quantize_tile(t):
+            for half in range(2):
+                words = x_sb[t, half].bitcast(F32)
+                bank = psum.tile([P, 2, 2, P], F32, name="bank", tag="bank")
+                for g in range(2):
+                    for u in range(2):
+                        nc.tensor.transpose(bank[:, g, u, :], words[:, 256 * g + u : 256 * (g + 1) : 2], ident[:])
+                grouped = work.tile([P, 2 * P * 4], BF16, name="grouped", align_bytes=64)
+                nc.scalar.copy(
+                    out=grouped[:].bitcast(F32).rearrange("p (g r u) -> p g r u", g=2, u=2),
+                    in_=bank[:].rearrange("p g u r -> p g r u"),
+                )
+                half_codes = keep.tile([P, 2 * P], U32, name="codes_%d_%d" % (t, half), align_bytes=64)
+                half_scales = keep.tile([P, 2 * P], U8, name="scales_%d_%d" % (t, half), align_bytes=64)
+                nc.vector.quantize_mx(out=half_codes[:].bitcast(E5M2X4), scales=half_scales[:], in_=grouped[:])
+                for g in range(2):
+                    codes[t, 2 * half + g] = half_codes[:, P * g : P * (g + 1)]
+                    x_scales[t, 2 * half + g] = half_scales[:, P * g : P * (g + 1)]
+
+        tables = keep.tile([P, 2, HALVES, PAIRS, 2, 2], F32, name="tables")
+
+        def build_tables():
+            gains = psum.tile([P, CHUNK], F32, name="gains", tag="bank")
+            nc.tensor.matmul(out=gains[:, 0 : 2 * HD], lhsT=ones[:], rhs=gain_rows[:], start=True, stop=True)
+            nc.vector.tensor_scalar(out=freqs[:, 1, :, :, 0], in0=freqs[:, 0, :, :, 1], scalar1=-1.0, scalar2=None, op0=ALU.mult)
+            nc.vector.tensor_copy(out=freqs[:, 1, :, :, 1], in_=freqs[:, 0, :, :, 0])
+            for kind in range(2):
+                gain = gains[:, HD * kind : HD * (kind + 1)].rearrange("p (j c) -> p j c", c=2)
+                for h in range(HALVES):
+                    nc.vector.tensor_tensor(
+                        out=tables[:, kind, h],
+                        in0=freqs[:, :, h].rearrange("p c j e -> p j c e"),
+                        in1=gain.unsqueeze(3).to_broadcast([P, PAIRS, 2, 2]),
+                        op=ALU.mult,
+                    )
+
+        def store(t, c, result):
+            dst = outs[0][:, CHUNK * c : CHUNK * (c + 1)] if c < Q_CHUNKS else outs[c - Q_CHUNKS + 1]
+            nc.sync.dma_start(out=dst[P * t : P * (t + 1), :], in_=result[:])
+
+        def project(t, c):
+            acc = psum.tile([P, CHUNK], F32, name="acc", tag="bank")
+            plane = first_plane if c == 0 else rest_plane
+            col = 0 if c == 0 else CHUNK * (c - 1)
+            for g in range(PASSES):
+                nc.tensor.matmul_mx(
+                    out=acc[:],
+                    lhsT=codes[t, g].bitcast(E5M2X4),
+                    lhsT_scale=x_scales[t, g],
+                    rhs=w_sb[c][:, g, :].bitcast(E2M1X4),
+                    rhs_scale=plane[:, g, col : col + CHUNK],
+                    start=(g == 0),
+                    stop=(g == PASSES - 1),
+                )
+            result = keep.tile([P, CHUNK], F32, name="result_%d_%d" % (t, c))
+            if c == V_CHUNK:
+                nc.scalar.copy(out=result[:], in_=acc[:])
+                store(t, c, result)
+                return None
+            squares = work.tile([P, CHUNK], BF16, name="squares")
+            sums = work.tile([P, HEADS], F32, name="sums")
+            for head in range(HEADS):
+                cols = slice(HD * head, HD * (head + 1))
+                nc.scalar.activation(out=squares[:, cols], in_=acc[:, cols], func=ACT.Square, accum_out=sums[:, head : head + 1])
+            rstd = work.tile([P, HEADS], F32, name="rstd")
+            nc.scalar.activation(out=rstd[:], in_=sums[:], func=ACT.Abs_reciprocal_sqrt, scale=1.0 / HD, bias=eps[:])
+            return (t, c, acc, rstd, result)
+
+        def rotate(t, c, acc, rstd, result):
+            table = tables[:, 0 if c < Q_CHUNKS else 1, t % HALVES].rearrange("p j c e -> p (j c) e")
+            terms = work.tile([P, HEADS, HD, 2], F32, name="terms")
+            for head in range(HEADS):
+                nc.vector.scalar_tensor_tensor(
+                    out=terms[:, head],
+                    in0=acc[:, HD * head : HD * (head + 1)].unsqueeze(2).to_broadcast([P, HD, 2]),
+                    scalar=rstd[:, head : head + 1],
+                    in1=table,
+                    op0=ALU.mult,
+                    op1=ALU.mult,
+                )
+            by_pair = terms[:].rearrange("p h (j c) e -> p (h j) c e", c=2)
+            adder = nc.vector if c == V_CHUNK - 1 and t >= TILES - 2 else nc.gpsimd
+            adder.tensor_tensor(
+                out=result[:].rearrange("p (n e) -> p n e", e=2),
+                in0=by_pair[:, :, 0, :],
+                in1=by_pair[:, :, 1, :],
+                op=ALU.add,
+            )
+            store(t, c, result)
+
+        head_steps = [(0, 0), 1, 2, (1, 0), 3, (2, 0), (0, 1), (3, 0)]
+        rest_steps = [(t, c) for c in range(1, CHUNKS) for t in range(TILES) if (t, c) not in head_steps]
+
+        quantize_tile(0)
+        build_tables()
+        waiting = None
+        for step in head_steps + rest_steps:
+            if isinstance(step, int):
+                quantize_tile(step)
+                fresh = None
+            else:
+                fresh = project(*step)
+            if waiting is not None:
+                rotate(*waiting)
+            waiting = fresh

@@ -44,14 +44,17 @@ def tile_attention_pa_kernel(tc, x, freqs_cis, wqkv_words, wqkv_scales, q_norm_w
         ident = keep.tile([P, P], F32, name="ident")
         make_identity(nc, ident[:])
 
-        first_plane = keep.tile([P, PASSES, CHUNK], U8, name="first_plane", align_bytes=64)
-        rest_plane = keep.tile([P, PASSES, E - CHUNK], U8, name="rest_plane", align_bytes=64)
+        plane_chunks = [(0, 1), (1, 2), (2, CHUNKS)]
+        planes = [
+            keep.tile([P, PASSES, CHUNK * (hi - lo)], U8, name="plane_%d" % lo, align_bytes=64) for lo, hi in plane_chunks
+        ]
         gain_rows = keep.tile([P, 2 * HD], BF16, name="gain_rows")
         ones = keep.tile([P, P], BF16, name="ones")
-        nc.vector.memset(first_plane[:].bitcast(I32), 0)
+        nc.vector.memset(planes[0][:].bitcast(I32), 0)
         nc.vector.memset(gain_rows[:], 0.0)
         nc.vector.memset(ones[:], 1.0)
-        nc.vector.memset(rest_plane[:].bitcast(I32), 0)
+        for plane in planes[1:]:
+            nc.vector.memset(plane[:].bitcast(I32), 0)
 
         eps = keep.tile([P, 1], F32, name="eps")
         nc.scalar.activation(out=eps[:], in_=ones[:, 0:1], func=ACT.Abs_reciprocal_sqrt, scale=1.0 / (EPS * EPS))
@@ -59,37 +62,50 @@ def tile_attention_pa_kernel(tc, x, freqs_cis, wqkv_words, wqkv_scales, q_norm_w
         x_sb = {}
         w_sb = {}
 
-        def load_x(t, pieces):
-            width = D // pieces
-            for i in range(pieces):
-                piece = keep.tile([P, width], BF16, name="x_%d_%d" % (t, i))
-                nc.sync.dma_start(out=piece[:], in_=x_rows[P * t : P * (t + 1), width * i : width * (i + 1)])
-                for j in range(width // 1024):
-                    x_sb[t, i * (width // 1024) + j] = piece[:, 1024 * j : 1024 * (j + 1)]
+        def load_x(t, lo, hi):
+            piece = keep.tile([P, 1024 * (hi - lo)], BF16, name="x_%d_%d" % (t, lo))
+            nc.sync.dma_start(out=piece[:], in_=x_rows[P * t : P * (t + 1), 1024 * lo : 1024 * hi])
+            for half in range(lo, hi):
+                x_sb[t, half] = piece[:, 1024 * (half - lo) : 1024 * (half - lo + 1)]
 
-        def load_w(c):
-            w_sb[c] = keep.tile([P, PASSES, 2 * CHUNK], U8, name="w_%d" % c, align_bytes=64)
-            src = wqkv_words[:, :, 2 * CHUNK * c : 2 * CHUNK * (c + 1)].rearrange("g p n -> p g n")
-            nc.sync.dma_start(out=w_sb[c][:].bitcast(I32), in_=src.bitcast(I32))
+        def load_w(chunks, passes):
+            width = 2 * CHUNK
+            piece = keep.tile([P, len(passes), width * len(chunks)], U8, name="w_%d_%d" % (chunks[0], passes[0]), align_bytes=64)
+            src = wqkv_words[passes[0] : passes[-1] + 1, :, width * chunks[0] : width * (chunks[-1] + 1)]
+            nc.sync.dma_start(out=piece[:].bitcast(I32), in_=src.rearrange("g p n -> p g n").bitcast(I32))
+            for i, c in enumerate(chunks):
+                for j, g in enumerate(passes):
+                    w_sb[c, g] = piece[:, j, width * i : width * (i + 1)]
 
-        def load_scales(plane, cols):
+        w_scales = {}
+
+        def load_scales(i):
+            lo, hi = plane_chunks[i]
             for r in range(4):
-                src = wqkv_scales[:, r:16:4, cols].rearrange("g q n -> q g n")
-                nc.sync.dma_start(out=plane[r:P:32, :, :].bitcast(I32), in_=src.bitcast(I32))
+                src = wqkv_scales[:, r:16:4, CHUNK * lo : CHUNK * hi].rearrange("g q n -> q g n")
+                nc.sync.dma_start(out=planes[i][r:P:32, :, :].bitcast(I32), in_=src.bitcast(I32))
+            for c in range(lo, hi):
+                for g in range(PASSES):
+                    w_scales[c, g] = planes[i][:, g, CHUNK * (c - lo) : CHUNK * (c - lo + 1)]
 
         freqs = keep.tile([P, 2, HALVES, PAIRS, 2], BF16, name="freqs")
 
-        load_x(0, 2)
-        load_w(0)
-        load_scales(first_plane, slice(0, CHUNK))
+        load_x(0, 0, 1)
+        load_w([0], [0, 1])
+        load_x(0, 1, 2)
+        load_scales(0)
+        load_w([0], [2, 3])
+        nc.sync.dma_start(out=freqs[:, 0], in_=freqs_cis.rearrange("(h p) j e -> p h j e", p=P))
+        load_x(1, 0, 2)
         nc.sync.dma_start(out=gain_rows[0:1, 0:HD], in_=q_norm_w.rearrange("(o d) -> o d", o=1))
         nc.sync.dma_start(out=gain_rows[0:1, HD : 2 * HD], in_=k_norm_w.rearrange("(o d) -> o d", o=1))
-        nc.sync.dma_start(out=freqs[:, 0], in_=freqs_cis.rearrange("(h p) j e -> p h j e", p=P))
-        for t in range(1, TILES):
-            load_x(t, 1)
-        load_scales(rest_plane, slice(CHUNK, E))
-        for c in range(1, CHUNKS):
-            load_w(c)
+        for t in range(2, TILES):
+            load_x(t, 0, 2)
+        load_scales(1)
+        load_w([1], range(PASSES))
+        load_scales(2)
+        for c in range(2, CHUNKS, 2):
+            load_w([c, c + 1], range(PASSES))
 
         codes = {}
         x_scales = {}
@@ -113,45 +129,44 @@ def tile_attention_pa_kernel(tc, x, freqs_cis, wqkv_words, wqkv_scales, q_norm_w
                     codes[t, 2 * half + g] = half_codes[:, P * g : P * (g + 1)]
                     x_scales[t, 2 * half + g] = half_scales[:, P * g : P * (g + 1)]
 
-        tables = keep.tile([P, 2, HALVES, PAIRS, 2, 2], F32, name="tables")
+        tables = {}
 
-        def build_tables():
-            gains = psum.tile([P, CHUNK], F32, name="gains", tag="bank")
-            nc.tensor.matmul(out=gains[:, 0 : 2 * HD], lhsT=ones[:], rhs=gain_rows[:], start=True, stop=True)
-            nc.vector.tensor_scalar(out=freqs[:, 1, :, :, 0], in0=freqs[:, 0, :, :, 1], scalar1=-1.0, scalar2=None, op0=ALU.mult)
-            nc.vector.tensor_copy(out=freqs[:, 1, :, :, 1], in_=freqs[:, 0, :, :, 0])
-            for kind in range(2):
-                gain = gains[:, HD * kind : HD * (kind + 1)].rearrange("p (j c) -> p j c", c=2)
-                for h in range(HALVES):
-                    nc.vector.tensor_tensor(
-                        out=tables[:, kind, h],
-                        in0=freqs[:, :, h].rearrange("p c j e -> p j c e"),
-                        in1=gain.unsqueeze(3).to_broadcast([P, PAIRS, 2, 2]),
-                        op=ALU.mult,
-                    )
+        def spread_gains():
+            spread = psum.tile([P, CHUNK], F32, name="spread", tag="bank")
+            nc.tensor.matmul(out=spread[:, 0 : 2 * HD], lhsT=ones[:], rhs=gain_rows[:], start=True, stop=True)
+            return spread
 
-        def store(t, c, result):
+        def build_table(gains, kind, h):
+            table = keep.tile([P, PAIRS, 2, 2], F32, name="table_%d_%d" % (kind, h))
+            gain = gains[:, HD * kind : HD * (kind + 1)].rearrange("p (j c) -> p j c", c=2)
+            nc.vector.tensor_tensor(
+                out=table[:],
+                in0=freqs[:, :, h].rearrange("p c j e -> p j c e"),
+                in1=gain.unsqueeze(3).to_broadcast([P, PAIRS, 2, 2]),
+                op=ALU.mult,
+            )
+            tables[kind, h] = table[:].rearrange("p j c e -> p (j c) e")
+
+        def store(queue, t, c, result):
             dst = outs[0][:, CHUNK * c : CHUNK * (c + 1)] if c < Q_CHUNKS else outs[c - Q_CHUNKS + 1]
-            nc.sync.dma_start(out=dst[P * t : P * (t + 1), :], in_=result[:])
+            queue.dma_start(out=dst[P * t : P * (t + 1), :], in_=result[:])
 
         def project(t, c):
             acc = psum.tile([P, CHUNK], F32, name="acc", tag="bank")
-            plane = first_plane if c == 0 else rest_plane
-            col = 0 if c == 0 else CHUNK * (c - 1)
             for g in range(PASSES):
                 nc.tensor.matmul_mx(
                     out=acc[:],
                     lhsT=codes[t, g].bitcast(E5M2X4),
                     lhsT_scale=x_scales[t, g],
-                    rhs=w_sb[c][:, g, :].bitcast(E2M1X4),
-                    rhs_scale=plane[:, g, col : col + CHUNK],
+                    rhs=w_sb[c, g].bitcast(E2M1X4),
+                    rhs_scale=w_scales[c, g],
                     start=(g == 0),
                     stop=(g == PASSES - 1),
                 )
             result = keep.tile([P, CHUNK], F32, name="result_%d_%d" % (t, c))
             if c == V_CHUNK:
                 nc.scalar.copy(out=result[:], in_=acc[:])
-                store(t, c, result)
+                store(nc.scalar, t, c, result)
                 return None
             squares = work.tile([P, CHUNK], BF16, name="squares")
             sums = work.tile([P, HEADS], F32, name="sums")
@@ -163,7 +178,7 @@ def tile_attention_pa_kernel(tc, x, freqs_cis, wqkv_words, wqkv_scales, q_norm_w
             return (t, c, acc, rstd, result)
 
         def rotate(t, c, acc, rstd, result):
-            table = tables[:, 0 if c < Q_CHUNKS else 1, t % HALVES].rearrange("p j c e -> p (j c) e")
+            table = tables[0 if c < Q_CHUNKS else 1, t % HALVES]
             terms = work.tile([P, HEADS, HD, 2], F32, name="terms")
             for head in range(HEADS):
                 nc.vector.scalar_tensor_tensor(
@@ -182,14 +197,22 @@ def tile_attention_pa_kernel(tc, x, freqs_cis, wqkv_words, wqkv_scales, q_norm_w
                 in1=by_pair[:, :, 1, :],
                 op=ALU.add,
             )
-            store(t, c, result)
-
-        head_steps = [(0, 0), 1, 2, (1, 0), 3, (2, 0), (0, 1), (3, 0)]
-        rest_steps = [(t, c) for c in range(1, CHUNKS) for t in range(TILES) if (t, c) not in head_steps]
+            store(nc.sync, t, c, result)
 
         quantize_tile(0)
-        build_tables()
+        nc.vector.tensor_scalar(out=freqs[:, 1, :, :, 0], in0=freqs[:, 0, :, :, 1], scalar1=-1.0, scalar2=None, op0=ALU.mult)
+        nc.vector.tensor_copy(out=freqs[:, 1, :, :, 1], in_=freqs[:, 0, :, :, 0])
+        waiting = project(0, 0)
+        gains = spread_gains()
+        for kind in range(2):
+            for h in range(HALVES):
+                build_table(gains, kind, h)
+        quantize_tile(1)
+        rotate(*waiting)
         waiting = None
+
+        head_steps = [2, (1, 0), 3, (2, 0), (0, 1), (3, 0)]
+        rest_steps = [(t, c) for c in range(1, CHUNKS) for t in range(TILES) if (t, c) not in head_steps]
         for step in head_steps + rest_steps:
             if isinstance(step, int):
                 quantize_tile(step)

@@ -37,12 +37,9 @@ def tile_attention_pa_kernel(tc, x, freqs_cis, wqkv_words, wqkv_scales, q_norm_w
 
     with ExitStack() as ctx:
         keep = ctx.enter_context(tc.tile_pool(name="keep", bufs=1))
-        work = ctx.enter_context(tc.tile_pool(name="work", bufs=4))
+        work = ctx.enter_context(tc.tile_pool(name="work", bufs=6))
         psum = ctx.enter_context(tc.psum_pool(name="psum", bufs=8))
         ctx.enter_context(tc.manual_schedule())
-
-        ident = keep.tile([P, P], F32, name="ident")
-        make_identity(nc, ident[:])
 
         plane_chunks = [(0, 1), (1, 2), (2, CHUNKS)]
         planes = [
@@ -50,7 +47,9 @@ def tile_attention_pa_kernel(tc, x, freqs_cis, wqkv_words, wqkv_scales, q_norm_w
         ]
         gain_rows = keep.tile([P, 2 * HD], BF16, name="gain_rows")
         ones = keep.tile([P, P], BF16, name="ones")
-        nc.vector.memset(planes[0][:].bitcast(I32), 0)
+        nc.gpsimd.memset(planes[0][:].bitcast(I32), 0)
+        ident = keep.tile([P, P], F32, name="ident")
+        make_identity(nc, ident[:])
         nc.vector.memset(gain_rows[:], 0.0)
         nc.vector.memset(ones[:], 1.0)
         for plane in planes[1:]:
@@ -91,9 +90,9 @@ def tile_attention_pa_kernel(tc, x, freqs_cis, wqkv_words, wqkv_scales, q_norm_w
         freqs = keep.tile([P, 2, HALVES, PAIRS, 2], BF16, name="freqs")
 
         load_x(0, 0, 1)
-        load_w([0], [0, 1])
-        load_x(0, 1, 2)
         load_scales(0)
+        load_x(0, 1, 2)
+        load_w([0], [0, 1])
         load_w([0], [2, 3])
         nc.sync.dma_start(out=freqs[:, 0], in_=freqs_cis.rearrange("(h p) j e -> p h j e", p=P))
         load_x(1, 0, 2)
@@ -147,27 +146,28 @@ def tile_attention_pa_kernel(tc, x, freqs_cis, wqkv_words, wqkv_scales, q_norm_w
             )
             tables[kind, h] = table[:].rearrange("p j c e -> p (j c) e")
 
-        def store(queue, t, c, result):
-            dst = outs[0][:, CHUNK * c : CHUNK * (c + 1)] if c < Q_CHUNKS else outs[c - Q_CHUNKS + 1]
-            queue.dma_start(out=dst[P * t : P * (t + 1), :], in_=result[:])
-
-        def project(t, c):
-            acc = psum.tile([P, CHUNK], F32, name="acc", tag="bank")
+        def multiply(t, c, cols):
+            acc = psum.tile([P, cols.stop - cols.start], F32, name="acc", tag="bank")
             for g in range(PASSES):
                 nc.tensor.matmul_mx(
                     out=acc[:],
                     lhsT=codes[t, g].bitcast(E5M2X4),
                     lhsT_scale=x_scales[t, g],
-                    rhs=w_sb[c, g].bitcast(E2M1X4),
-                    rhs_scale=w_scales[c, g],
+                    rhs=w_sb[c, g][:, 2 * cols.start : 2 * cols.stop].bitcast(E2M1X4),
+                    rhs_scale=w_scales[c, g][:, cols],
                     start=(g == 0),
                     stop=(g == PASSES - 1),
                 )
-            result = keep.tile([P, CHUNK], F32, name="result_%d_%d" % (t, c))
-            if c == V_CHUNK:
-                nc.scalar.copy(out=result[:], in_=acc[:])
-                store(nc.scalar, t, c, result)
-                return None
+            return acc
+
+        def project_v(queue, t, cols):
+            acc = multiply(t, V_CHUNK, cols)
+            result = keep.tile([P, cols.stop - cols.start], F32, name="v_%d_%d" % (t, cols.start))
+            nc.scalar.copy(out=result[:], in_=acc[:])
+            queue.dma_start(out=outs[2][P * t : P * (t + 1), cols], in_=result[:])
+
+        def project(t, c):
+            acc = multiply(t, c, slice(0, CHUNK))
             squares = work.tile([P, CHUNK], BF16, name="squares")
             sums = work.tile([P, HEADS], F32, name="sums")
             for head in range(HEADS):
@@ -175,11 +175,10 @@ def tile_attention_pa_kernel(tc, x, freqs_cis, wqkv_words, wqkv_scales, q_norm_w
                 nc.scalar.activation(out=squares[:, cols], in_=acc[:, cols], func=ACT.Square, accum_out=sums[:, head : head + 1])
             rstd = work.tile([P, HEADS], F32, name="rstd")
             nc.scalar.activation(out=rstd[:], in_=sums[:], func=ACT.Abs_reciprocal_sqrt, scale=1.0 / HD, bias=eps[:])
-            return (t, c, acc, rstd, result)
+            return (t, c, acc, rstd)
 
-        def rotate(t, c, acc, rstd, result):
+        def rotation_terms(terms, t, c, acc, rstd):
             table = tables[0 if c < Q_CHUNKS else 1, t % HALVES]
-            terms = work.tile([P, HEADS, HD, 2], F32, name="terms")
             for head in range(HEADS):
                 nc.vector.scalar_tensor_tensor(
                     out=terms[:, head],
@@ -189,15 +188,38 @@ def tile_attention_pa_kernel(tc, x, freqs_cis, wqkv_words, wqkv_scales, q_norm_w
                     op0=ALU.mult,
                     op1=ALU.mult,
                 )
-            by_pair = terms[:].rearrange("p h (j c) e -> p (h j) c e", c=2)
-            adder = nc.vector if c == V_CHUNK - 1 and t >= TILES - 2 else nc.gpsimd
+
+        def add_terms(adder, result, terms):
+            by_pair = terms.rearrange("p h (j c) e -> p (h j) c e", c=2)
             adder.tensor_tensor(
-                out=result[:].rearrange("p (n e) -> p n e", e=2),
+                out=result.rearrange("p (n e) -> p n e", e=2),
                 in0=by_pair[:, :, 0, :],
                 in1=by_pair[:, :, 1, :],
                 op=ALU.add,
             )
-            store(nc.sync, t, c, result)
+
+        wide_terms = {}
+
+        def rotate_q(t, c, acc, rstd):
+            chunks = 2 if c >= 2 and t < TILES - 1 else 1
+            side = c % chunks
+            if side == 0:
+                wide_terms[t] = work.tile([P, chunks * HEADS, HD, 2], F32, name="terms_%d" % chunks, bufs=6 // chunks)
+            rotation_terms(wide_terms[t][:, HEADS * side : HEADS * (side + 1)], t, c, acc, rstd)
+            if side == chunks - 1:
+                result = keep.tile([P, chunks * CHUNK], F32, name="q_%d_%d" % (t, c))
+                add_terms(nc.gpsimd, result[:], wide_terms[t][:])
+                nc.sync.dma_start(out=outs[0][P * t : P * (t + 1), CHUNK * (c - side) : CHUNK * (c + 1)], in_=result[:])
+
+        def k_terms(t, c, acc, rstd):
+            terms = work.tile([P, HEADS, HD, 2], F32, name="terms_1")
+            rotation_terms(terms[:], t, c, acc, rstd)
+            return terms
+
+        def finish_k(adder, t, terms):
+            result = keep.tile([P, CHUNK], F32, name="k_%d" % t)
+            add_terms(adder, result[:], terms[:])
+            nc.sync.dma_start(out=outs[1][P * t : P * (t + 1), :], in_=result[:])
 
         quantize_tile(0)
         nc.vector.tensor_scalar(out=freqs[:, 1, :, :, 0], in0=freqs[:, 0, :, :, 1], scalar1=-1.0, scalar2=None, op0=ALU.mult)
@@ -208,17 +230,29 @@ def tile_attention_pa_kernel(tc, x, freqs_cis, wqkv_words, wqkv_scales, q_norm_w
             for h in range(HALVES):
                 build_table(gains, kind, h)
         quantize_tile(1)
-        rotate(*waiting)
+        rotate_q(*waiting)
         waiting = None
 
-        head_steps = [2, (1, 0), 3, (2, 0), (0, 1), (3, 0)]
-        rest_steps = [(t, c) for c in range(1, CHUNKS) for t in range(TILES) if (t, c) not in head_steps]
-        for step in head_steps + rest_steps:
+        steps = [2, (1, 0), 3, (2, 0), (0, 1), (3, 0)]
+        steps += [(t, 1) for t in range(1, TILES)]
+        steps += [(t, c) for t in range(TILES) for c in (2, 3)]
+        for step in steps:
             if isinstance(step, int):
                 quantize_tile(step)
                 fresh = None
             else:
                 fresh = project(*step)
             if waiting is not None:
-                rotate(*waiting)
+                rotate_q(*waiting)
             waiting = fresh
+
+        k_banks = [project(0, Q_CHUNKS)]
+        rotate_q(*waiting)
+        k_banks += [project(t, Q_CHUNKS) for t in range(1, TILES)]
+        terms = [k_terms(*bank) for bank in k_banks]
+        for t in range(TILES - 1):
+            project_v(nc.scalar, t, slice(0, CHUNK))
+        for t in range(TILES):
+            finish_k(nc.gpsimd if t == 0 else nc.vector, t, terms[t])
+        project_v(nc.scalar, TILES - 1, slice(0, CHUNK // 2))
+        project_v(nc.scalar, TILES - 1, slice(CHUNK // 2, CHUNK))

from contextlib import ExitStack

import concourse.mybir as mybir
from concourse.masks import make_identity

B, S, D, NH, NKV, HD = 2, 256, 2048, 16, 4, 128
E = (NH + 2 * NKV) * HD
EPS = 1e-6
FLOPS = 2 * B * S * D * E

F32 = mybir.dt.float32
BF16 = mybir.dt.bfloat16
I32 = mybir.dt.int32
U32 = mybir.dt.uint32
U8 = mybir.dt.uint8
E5M2X4 = mybir.dt.float8_e5m2_x4
E2M1X4 = mybir.dt.float4_e2m1fn_x4
ACT = mybir.ActivationFunctionType
ALU = mybir.AluOpType

P = 128
PASSES = D // 512
CHUNK = 512
CHUNKS = E // CHUNK
Q_CHUNKS = NH * HD // CHUNK
V_CHUNK = CHUNKS - 1
HEADS = CHUNK // HD
TILES = B * S // P
HALVES = S // P
PAIRS = HD // 2


def tile_attention_pa_kernel(tc, x, freqs_cis, wqkv_words, wqkv_scales, q_norm_w, k_norm_w, out_0, out_1, out_2):
    nc = tc.nc
    x_rows = x.rearrange("b s d -> (b s) d")
    outs = [o.rearrange("b s h d -> (b s) (h d)") for o in (out_0, out_1, out_2)]

    with ExitStack() as ctx:
        keep = ctx.enter_context(tc.tile_pool(name="keep", bufs=1))
        work = ctx.enter_context(tc.tile_pool(name="work", bufs=6))
        psum = ctx.enter_context(tc.psum_pool(name="psum", bufs=8))
        ctx.enter_context(tc.manual_schedule())

        plane_chunks = [(0, 1), (1, 2), (2, CHUNKS)]
        planes = [
            keep.tile([P, PASSES, CHUNK * (hi - lo)], U8, name="plane_%d" % lo, align_bytes=64) for lo, hi in plane_chunks
        ]
        gain_rows = keep.tile([P, 2 * HD], BF16, name="gain_rows")
        ones = keep.tile([P, P], BF16, name="ones")
        nc.gpsimd.memset(planes[0][:].bitcast(I32), 0)
        ident = keep.tile([P, P], F32, name="ident")
        make_identity(nc, ident[:])
        nc.vector.memset(gain_rows[:], 0.0)
        nc.vector.memset(ones[:], 1.0)
        for plane in planes[1:]:
            nc.vector.memset(plane[:].bitcast(I32), 0)

        eps = keep.tile([P, 1], F32, name="eps")
        nc.scalar.activation(out=eps[:], in_=ones[:, 0:1], func=ACT.Abs_reciprocal_sqrt, scale=1.0 / (EPS * EPS))

        x_sb = {}
        w_sb = {}

        def load_x(t, lo, hi):
            piece = keep.tile([P, 1024 * (hi - lo)], BF16, name="x_%d_%d" % (t, lo))
            nc.sync.dma_start(out=piece[:], in_=x_rows[P * t : P * (t + 1), 1024 * lo : 1024 * hi])
            for half in range(lo, hi):
                x_sb[t, half] = piece[:, 1024 * (half - lo) : 1024 * (half - lo + 1)]

        def load_w(chunks, passes):
            width = 2 * CHUNK
            piece = keep.tile([P, len(passes), width * len(chunks)], U8, name="w_%d_%d" % (chunks[0], passes[0]), align_bytes=64)
            src = wqkv_words[passes[0] : passes[-1] + 1, :, width * chunks[0] : width * (chunks[-1] + 1)]
            nc.sync.dma_start(out=piece[:].bitcast(I32), in_=src.rearrange("g p n -> p g n").bitcast(I32))
            for i, c in enumerate(chunks):
                for j, g in enumerate(passes):
                    w_sb[c, g] = piece[:, j, width * i : width * (i + 1)]

        w_scales = {}

        def load_scales(i):
            lo, hi = plane_chunks[i]
            for r in range(4):
                src = wqkv_scales[:, r:16:4, CHUNK * lo : CHUNK * hi].rearrange("g q n -> q g n")
                nc.sync.dma_start(out=planes[i][r:P:32, :, :].bitcast(I32), in_=src.bitcast(I32))
            for c in range(lo, hi):
                for g in range(PASSES):
                    w_scales[c, g] = planes[i][:, g, CHUNK * (c - lo) : CHUNK * (c - lo + 1)]

        freqs = keep.tile([P, 2, HALVES, PAIRS, 2], BF16, name="freqs")

        load_x(0, 0, 1)
        load_scales(0)
        load_x(0, 1, 2)
        load_w([0], [0, 1])
        load_w([0], [2, 3])
        nc.sync.dma_start(out=freqs[:, 0], in_=freqs_cis.rearrange("(h p) j e -> p h j e", p=P))
        load_x(1, 0, 2)
        nc.sync.dma_start(out=gain_rows[0:1, 0:HD], in_=q_norm_w.rearrange("(o d) -> o d", o=1))
        nc.sync.dma_start(out=gain_rows[0:1, HD : 2 * HD], in_=k_norm_w.rearrange("(o d) -> o d", o=1))
        for t in range(2, TILES):
            load_x(t, 0, 2)
        load_scales(1)
        load_w([1], range(PASSES))
        load_scales(2)
        for c in range(2, CHUNKS, 2):
            load_w([c, c + 1], range(PASSES))

        codes = {}
        x_scales = {}

        def quantize_tile(t):
            for half in range(2):
                words = x_sb[t, half].bitcast(F32)
                bank = psum.tile([P, 2, 2, P], F32, name="bank", tag="bank")
                for g in range(2):
                    for u in range(2):
                        nc.tensor.transpose(bank[:, g, u, :], words[:, 256 * g + u : 256 * (g + 1) : 2], ident[:])
                grouped = work.tile([P, 2 * P * 4], BF16, name="grouped", align_bytes=64)
                nc.scalar.copy(
                    out=grouped[:].bitcast(F32).rearrange("p (g r u) -> p g r u", g=2, u=2),
                    in_=bank[:].rearrange("p g u r -> p g r u"),
                )
                half_codes = keep.tile([P, 2 * P], U32, name="codes_%d_%d" % (t, half), align_bytes=64)
                half_scales = keep.tile([P, 2 * P], U8, name="scales_%d_%d" % (t, half), align_bytes=64)
                nc.vector.quantize_mx(out=half_codes[:].bitcast(E5M2X4), scales=half_scales[:], in_=grouped[:])
                for g in range(2):
                    codes[t, 2 * half + g] = half_codes[:, P * g : P * (g + 1)]
                    x_scales[t, 2 * half + g] = half_scales[:, P * g : P * (g + 1)]

        tables = {}

        def spread_gains():
            spread = psum.tile([P, CHUNK], F32, name="spread", tag="bank")
            nc.tensor.matmul(out=spread[:, 0 : 2 * HD], lhsT=ones[:], rhs=gain_rows[:], start=True, stop=True)
            return spread

        def build_table(gains, kind, h):
            table = keep.tile([P, PAIRS, 2, 2], F32, name="table_%d_%d" % (kind, h))
            gain = gains[:, HD * kind : HD * (kind + 1)].rearrange("p (j c) -> p j c", c=2)
            nc.vector.tensor_tensor(
                out=table[:],
                in0=freqs[:, :, h].rearrange("p c j e -> p j c e"),
                in1=gain.unsqueeze(3).to_broadcast([P, PAIRS, 2, 2]),
                op=ALU.mult,
            )
            tables[kind, h] = table[:].rearrange("p j c e -> p (j c) e")

        def multiply(t, c, cols):
            acc = psum.tile([P, cols.stop - cols.start], F32, name="acc", tag="bank")
            for g in range(PASSES):
                nc.tensor.matmul_mx(
                    out=acc[:],
                    lhsT=codes[t, g].bitcast(E5M2X4),
                    lhsT_scale=x_scales[t, g],
                    rhs=w_sb[c, g][:, 2 * cols.start : 2 * cols.stop].bitcast(E2M1X4),
                    rhs_scale=w_scales[c, g][:, cols],
                    start=(g == 0),
                    stop=(g == PASSES - 1),
                )
            return acc

        def project_v(queue, t, cols):
            acc = multiply(t, V_CHUNK, cols)
            result = keep.tile([P, cols.stop - cols.start], F32, name="v_%d_%d" % (t, cols.start))
            nc.scalar.copy(out=result[:], in_=acc[:])
            queue.dma_start(out=outs[2][P * t : P * (t + 1), cols], in_=result[:])

        def project(t, c):
            acc = multiply(t, c, slice(0, CHUNK))
            squares = work.tile([P, CHUNK], BF16, name="squares")
            sums = work.tile([P, HEADS], F32, name="sums")
            for head in range(HEADS):
                cols = slice(HD * head, HD * (head + 1))
                nc.scalar.activation(out=squares[:, cols], in_=acc[:, cols], func=ACT.Square, accum_out=sums[:, head : head + 1])
            rstd = work.tile([P, HEADS], F32, name="rstd")
            nc.scalar.activation(out=rstd[:], in_=sums[:], func=ACT.Abs_reciprocal_sqrt, scale=1.0 / HD, bias=eps[:])
            return (t, c, acc, rstd)

        def rotation_terms(terms, t, c, acc, rstd):
            table = tables[0 if c < Q_CHUNKS else 1, t % HALVES]
            for head in range(HEADS):
                nc.vector.scalar_tensor_tensor(
                    out=terms[:, head],
                    in0=acc[:, HD * head : HD * (head + 1)].unsqueeze(2).to_broadcast([P, HD, 2]),
                    scalar=rstd[:, head : head + 1],
                    in1=table,
                    op0=ALU.mult,
                    op1=ALU.mult,
                )

        def add_terms(adder, result, terms):
            by_pair = terms.rearrange("p h (j c) e -> p (h j) c e", c=2)
            adder.tensor_tensor(
                out=result.rearrange("p (n e) -> p n e", e=2),
                in0=by_pair[:, :, 0, :],
                in1=by_pair[:, :, 1, :],
                op=ALU.add,
            )

        wide_terms = {}

        def rotate_q(t, c, acc, rstd):
            chunks = 2 if c >= 2 and t < TILES - 1 else 1
            side = c % chunks
            if side == 0:
                wide_terms[t] = work.tile([P, chunks * HEADS, HD, 2], F32, name="terms_%d" % chunks, bufs=6 // chunks)
            rotation_terms(wide_terms[t][:, HEADS * side : HEADS * (side + 1)], t, c, acc, rstd)
            if side == chunks - 1:
                result = keep.tile([P, chunks * CHUNK], F32, name="q_%d_%d" % (t, c))
                add_terms(nc.gpsimd, result[:], wide_terms[t][:])
                nc.sync.dma_start(out=outs[0][P * t : P * (t + 1), CHUNK * (c - side) : CHUNK * (c + 1)], in_=result[:])

        def k_terms(t, c, acc, rstd):
            terms = work.tile([P, HEADS, HD, 2], F32, name="terms_1")
            rotation_terms(terms[:], t, c, acc, rstd)
            return terms

        def finish_k(adder, t, terms):
            result = keep.tile([P, CHUNK], F32, name="k_%d" % t)
            add_terms(adder, result[:], terms[:])
            nc.sync.dma_start(out=outs[1][P * t : P * (t + 1), :], in_=result[:])

        quantize_tile(0)
        nc.vector.tensor_scalar(out=freqs[:, 1, :, :, 0], in0=freqs[:, 0, :, :, 1], scalar1=-1.0, scalar2=None, op0=ALU.mult)
        nc.vector.tensor_copy(out=freqs[:, 1, :, :, 1], in_=freqs[:, 0, :, :, 0])
        waiting = project(0, 0)
        gains = spread_gains()
        for kind in range(2):
            for h in range(HALVES):
                build_table(gains, kind, h)
        quantize_tile(1)
        rotate_q(*waiting)
        waiting = None

        steps = [2, (1, 0), 3, (2, 0), (0, 1), (3, 0)]
        steps += [(t, 1) for t in range(1, TILES)]
        steps += [(t, c) for t in range(TILES) for c in (2, 3)]
        for step in steps:
            if isinstance(step, int):
                quantize_tile(step)
                fresh = None
            else:
                fresh = project(*step)
            if waiting is not None:
                rotate_q(*waiting)
            waiting = fresh

        k_banks = [project(0, Q_CHUNKS)]
        rotate_q(*waiting)
        k_banks += [project(t, Q_CHUNKS) for t in range(1, TILES)]
        terms = [k_terms(*bank) for bank in k_banks]
        for t in range(TILES - 1):
            project_v(nc.scalar, t, slice(0, CHUNK))
        for t in range(TILES):
            finish_k(nc.gpsimd if t == 0 else nc.vector, t, terms[t])
        project_v(nc.scalar, TILES - 1, slice(0, CHUNK // 2))
        project_v(nc.scalar, TILES - 1, slice(CHUNK // 2, CHUNK))
